import numpy as np
import ml_dtypes


def mxq(x, axis, fmt="e4m3"):
    dtype, down = {"e4m3": (ml_dtypes.float8_e4m3fn, 7), "e5m2": (ml_dtypes.float8_e5m2, 14)}[fmt]
    v = np.moveaxis(np.asarray(x, np.float32).astype(ml_dtypes.bfloat16).astype(np.float64), axis, -1)
    blocks = v.reshape(v.shape[:-1] + (-1, 32))
    amax = np.abs(blocks).max(-1, keepdims=True)
    byte = np.maximum(np.where(amax > 0, np.frexp(amax)[1] - 1 + 127, 0) - down, 1)
    scale = np.exp2(byte - 127.0)
    codes = (blocks / scale).astype(np.float32).astype(dtype).astype(np.float64)
    return np.moveaxis((codes * scale).reshape(v.shape), -1, axis)


WIDE = False


def mx_kscale(k):
    if not WIDE:
        return np.ones(k)
    levels = np.array([30, -30])
    if k % 512:
        return np.exp2(np.random.permutation(np.resize(levels, k // 32))).repeat(32)
    a = np.empty((k // 512, 16))
    for p in range(k // 512):
        a[p, :8] = np.random.permutation(np.resize(levels, 8))
        for g in range(8):
            far = levels[np.abs(levels - a[p, g]) >= 10]
            a[p, g + 8] = far[np.random.randint(len(far))]
    return np.exp2(a.ravel()).repeat(32)


BF16 = ml_dtypes.bfloat16


def bf(x):
    return np.asarray(x, np.float32).astype(BF16)


def f64(x):
    return np.asarray(x).astype(np.float64)


E2M1 = np.array([0.0, 0.5, 1.0, 1.5, 2.0, 3.0, 4.0, 6.0, -0.0, -0.5, -1.0, -1.5, -2.0, -3.0, -4.0, -6.0])


def pack_weight(w, fmt):
    k, n = w.shape
    w = f64(bf(w)).reshape(k // 32, 32, n)
    amax = np.abs(w).max(1)
    if fmt == "e4m3":
        byte = np.frexp(amax)[1] - 1 + 127 - 7
    else:
        mant, ex = np.frexp(amax / 6.0)
        byte = np.where(mant > 0.5, ex, ex - 1) + 127
    byte = np.clip(np.where(amax > 0, byte, 1), 1, 254)
    scaled = (w * np.exp2(127.0 - byte)[:, None, :]).reshape(k, n).astype(np.float32)
    by_word = np.ascontiguousarray(scaled.reshape(k // 512, 128, 4, n).transpose(0, 1, 3, 2))
    if fmt == "e4m3":
        words = by_word.astype(ml_dtypes.float8_e4m3fn).view(np.uint8)
    else:
        c = by_word.astype(ml_dtypes.float4_e2m1fn).view(np.uint8) & 0xF
        words = c[..., 0::2] | (c[..., 1::2] << 4)
    return np.ascontiguousarray(words), np.ascontiguousarray(byte.astype(np.uint8).reshape(k // 512, 16, n))


def unpack_weight(words, scales, fmt):
    g, p, n, _ = words.shape
    if fmt == "e4m3":
        vals = np.ascontiguousarray(words).view(ml_dtypes.float8_e4m3fn).astype(np.float64)
    else:
        nib = np.empty((g, p, n, 4), np.uint8)
        nib[..., 0::2] = words & 0xF
        nib[..., 1::2] = words >> 4
        vals = E2M1[nib]
    vals = vals * np.repeat(np.exp2(scales.astype(np.float64) - 127.0), 8, axis=1)[..., None]
    return vals.transpose(0, 1, 3, 2).reshape(g * 512, n)

def pack4(w):
    words, scales = pack_weight(w, "e2m1")
    return words.reshape(words.shape[0], 128, -1), scales


def unpack4(words, scales):
    return unpack_weight(words.reshape(words.shape[0], 128, -1, 2), scales, "e2m1")


B, F, H, W, NH, DH, P, SINK, LOCAL = 1, 4, 16, 32, 8, 128, 1024, 1, 2
D = NH * DH
L = F * H * W
C = DH // 2
C1 = C // 3
C0 = C - 2 * C1
THETA = 1.0e4
EPS = 1.0e-6


def rope_params(n):
    inv = 1.0 / THETA ** (np.arange(0, 2 * n, 2) / (2 * n))
    ang = np.outer(np.arange(P), inv)
    return np.stack([np.cos(ang), np.sin(ang)], -1)


def setup_inputs():
    s = mx_kscale(D)
    freqs = np.concatenate([rope_params(C0), rope_params(C1), rope_params(C1)], axis=1)
    x = bf(np.random.standard_normal((B, L, D)) * s)
    wq_words, wq_scales = pack4((np.random.standard_normal((D, D)) / np.sqrt(D) / s).T)
    bq = bf(np.random.standard_normal(D) * 0.3)
    wk_words, wk_scales = pack4((np.random.standard_normal((D, D)) / np.sqrt(D) / s).T)
    bk = bf(np.random.standard_normal(D) * 0.3)
    gq = bf(1.5 * (1.0 + 0.1 * np.random.standard_normal(D)))
    gk = bf(1.5 * (1.0 + 0.1 * np.random.standard_normal(D)))
    return {
        "x": x,
        "wq_words": wq_words,
        "wq_scales": wq_scales,
        "bq": bq,
        "wk_words": wk_words,
        "wk_scales": wk_scales,
        "bk": bk,
        "gq": gq,
        "gk": gk,
        "freqs": bf(freqs),
    }


def rmsnorm(t, g):
    return t * (1.0 / np.sqrt(np.mean(t * t, -1, keepdims=True) + EPS)) * g


def rope_table(fr):
    ft = np.broadcast_to(fr[:F, :C0].reshape(F, 1, 1, C0, 2), (F, H, W, C0, 2))
    fh = np.broadcast_to(fr[:H, C0:C0 + C1].reshape(1, H, 1, C1, 2), (F, H, W, C1, 2))
    fw = np.broadcast_to(fr[:W, C0 + C1:].reshape(1, 1, W, C1, 2), (F, H, W, C1, 2))
    return np.concatenate([ft, fh, fw], -2).reshape(L, C, 2)


def apply_rope(t, fr):
    tr = t.reshape(B, L, NH, C, 2)
    a, b = tr[..., 0], tr[..., 1]
    cos = fr[None, :, None, :, 0]
    sin = fr[None, :, None, :, 1]
    return np.stack([a * cos - b * sin, a * sin + b * cos], -1).reshape(B, L, NH, DH)


def reference(x, wq_words, wq_scales, bq, wk_words, wk_scales, bk, gq, gk, freqs):
    xq = mxq(f64(x), 2, "e5m2")
    q = rmsnorm((xq @ unpack4(wq_words, wq_scales)) + f64(bq), f64(gq))
    k = rmsnorm((xq @ unpack4(wk_words, wk_scales)) + f64(bk), f64(gk))
    fr = rope_table(f64(freqs))
    return apply_rope(q, fr), apply_rope(k, fr)

@@ -1,0 +1,351 @@
+from contextlib import ExitStack
+
+import concourse.mybir as mybir
+from concourse.masks import make_identity
+
+F32 = mybir.dt.float32
+BF16 = mybir.dt.bfloat16
+I32 = mybir.dt.int32
+U32 = mybir.dt.uint32
+U8 = mybir.dt.uint8
+E5M2X4 = mybir.dt.float8_e5m2_x4
+E2M1X4 = mybir.dt.float4_e2m1fn_x4
+ACT = mybir.ActivationFunctionType
+ALU = mybir.AluOpType
+
+P = 128
+L, D, NH, DH = 2048, 1024, 8, 128
+FRAMES, ROWS, COLS = 4, 16, 32
+EPS = 1.0e-6
+PASSES = D // 512
+TILES = L // P
+ROWS_PER_TILE = P // COLS
+ROW_GROUPS = ROWS // ROWS_PER_TILE
+WF, WH, WW = 44, 42, 42
+BLOCK = 2
+NTOK = BLOCK * P
+BLOCKS = TILES // BLOCK
+HEADS_PER_FILL = 512 // NTOK
+FILLS = NH // HEADS_PER_FILL
+UNITS = 2 * TILES
+FREQ_ROW = 32
+ANG_F, ANG_H, ANG_W = 0, FRAMES * WF, FRAMES * WF + ROW_GROUPS * WH
+ANG = ANG_W + WW
+
+FLOPS = 2 * L * D * 2 * D
+
+
+def tile_causalwanselfattention_pa_kernel(
+    tc, x, wq_words, wq_scales, bq, wk_words, wk_scales, bk, gq, gk, freqs, out_0, out_1
+):
+    nc = tc.nc
+    outs = [o.rearrange("b l h d -> (b l) (h d)") for o in (out_0, out_1)]
+    x_rows = x.rearrange("b (i t p) d -> (b i) p t d", p=P, t=BLOCK)
+
+    with ExitStack() as ctx:
+        keep = ctx.enter_context(tc.tile_pool(name="keep", bufs=1))
+        work = ctx.enter_context(tc.tile_pool(name="work", bufs=3))
+        mx_psum = ctx.enter_context(tc.psum_pool(name="mx_psum", bufs=3))
+        z_psum = ctx.enter_context(tc.psum_pool(name="z_psum", bufs=5))
+        ctx.enter_context(tc.manual_schedule())
+
+        small = keep.tile([P, DH], BF16, name="small")
+        nc.vector.memset(small[64:P, :], 0.0)
+        nc.sync.dma_start(
+            out=small[FREQ_ROW : FREQ_ROW + COLS, :], in_=freqs[0:COLS].rearrange("r j c -> r (j c)")
+        )
+        for row, vec in ((16, gq), (24, gk), (0, bq), (8, bk)):
+            nc.sync.dma_start(out=small[row : row + NH, :], in_=vec.rearrange("(h n) -> h n", n=DH))
+        x_sb = [keep.tile([P, BLOCK, D], BF16, name="x%d" % i) for i in range(BLOCKS)]
+        nc.sync.dma_start(out=x_sb[0][:], in_=x_rows[0])
+        w_words, w_planes = [], []
+        for m, (words, scales) in enumerate(((wq_words, wq_scales), (wk_words, wk_scales))):
+            plane = keep.tile([P, PASSES, D], U8, name="plane%d" % m, align_bytes=64)
+            for quad in range(4):
+                nc.sync.dma_start(
+                    out=plane[32 * quad : 32 * quad + 4, :, :].bitcast(I32),
+                    in_=scales[:, 4 * quad : 4 * quad + 4, :].rearrange("g r n -> r g n").bitcast(I32),
+                )
+            codes = keep.tile([P, PASSES, 2 * D], U8, name="words%d" % m, align_bytes=64)
+            nc.sync.dma_start(out=codes[:].bitcast(I32), in_=words.rearrange("g p n -> p g n").bitcast(I32))
+            w_words.append(codes)
+            w_planes.append(plane)
+            nc.sync.dma_start(out=x_sb[1 + m][:], in_=x_rows[1 + m])
+        for i in range(3, BLOCKS):
+            nc.sync.dma_start(out=x_sb[i][:], in_=x_rows[i])
+
+        ident_bf = keep.tile([P, P], BF16, name="ident_bf")
+        make_identity(nc, ident_bf[:])
+        ident = keep.tile([P, P], F32, name="ident")
+        make_identity(nc, ident[:])
+        sign = keep.tile([P, 2, 2], F32, name="sign")
+        nc.vector.memset(sign[:], 1.0)
+        nc.vector.memset(sign[:, 1, 1:2], -1.0)
+        half_eps = keep.tile([P, UNITS, 2], F32, name="half_eps")
+        nc.vector.tensor_scalar(
+            out=half_eps[:, :, 1:2],
+            in0=sign[:, 0, 0:1].unsqueeze(1).broadcast_to([P, UNITS, 1]),
+            scalar1=EPS,
+            scalar2=None,
+            op0=ALU.mult,
+        )
+        half_b = keep.tile([P, UNITS], F32, name="half_b")
+        half_a = keep.tile([P, UNITS], F32, name="half_a")
+        rstd = keep.tile([P, UNITS], F32, name="rstd")
+        sel_h = keep.tile([P, ROWS, COLS], BF16, name="sel_h")
+        nc.vector.tensor_copy(
+            out=sel_h[:], in_=ident_bf[:, FREQ_ROW : FREQ_ROW + ROWS].unsqueeze(2).broadcast_to([P, ROWS, COLS])
+        )
+        sel_w = keep.tile([P, ROWS_PER_TILE, COLS], BF16, name="sel_w")
+        nc.vector.tensor_copy(
+            out=sel_w[:],
+            in_=ident_bf[:, FREQ_ROW : FREQ_ROW + COLS].unsqueeze(1).broadcast_to([P, ROWS_PER_TILE, COLS]),
+        )
+
+        def row_to_all(row):
+            return ident_bf[:, row : row + 1].to_broadcast([P, P])
+
+        ang = mx_psum.tile([P, 512], F32, name="ang", tag="mx")
+        for f in range(FRAMES):
+            nc.tensor.matmul(
+                out=ang[:, ANG_F + WF * f : ANG_F + WF * (f + 1)], lhsT=row_to_all(FREQ_ROW + f),
+                rhs=small[:, 0:WF], start=True, stop=True,
+            )
+        for r in range(ROW_GROUPS):
+            nc.tensor.matmul(
+                out=ang[:, ANG_H + WH * r : ANG_H + WH * (r + 1)],
+                lhsT=sel_h[:, ROWS_PER_TILE * r : ROWS_PER_TILE * (r + 1), :].rearrange("p a b -> p (a b)"),
+                rhs=small[:, WF : WF + WH], start=True, stop=True,
+            )
+        nc.tensor.matmul(
+            out=ang[:, ANG_W:ANG], lhsT=sel_w[:].rearrange("p a b -> p (a b)"),
+            rhs=small[:, WF + WH : DH], start=True, stop=True,
+        )
+        cs = keep.tile([P, 2, ANG], F32, name="cs")
+        shape = [P, 2, ANG // 2, 2]
+        nc.vector.tensor_tensor(
+            out=cs[:].rearrange("p c (j e) -> p c j e", e=2),
+            in0=ang[:, 0:ANG].rearrange("p (j c) -> p c j", c=2).unsqueeze(3).broadcast_to(shape),
+            in1=sign[:].unsqueeze(2).broadcast_to(shape),
+            op=ALU.mult,
+        )
+
+        gain = []
+
+        def spread_gain(m):
+            bank = z_psum.tile([P, NH, DH], BF16, name="gain%d" % m, tag="z")
+            for h in range(NH):
+                nc.tensor.matmul(
+                    out=bank[:, h, :], lhsT=row_to_all(16 + NH * m + h), rhs=small[:], start=True, stop=True
+                )
+            gain.append(bank)
+
+        tables = {}
+
+        def make_table(eng, gsrc, m, part, variant):
+            col, width, base = ((0, WF, ANG_F), (WF, WH, ANG_H), (WF + WH, WW, ANG_W))[part]
+            tab = keep.tile([P, 2, NH, width], F32, name="tab%d_%d_%d" % (m, part, variant))
+            shape = [P, 2, NH, width]
+            eng.tensor_tensor(
+                out=tab[:],
+                in0=gsrc[:, :, col : col + width].unsqueeze(1).broadcast_to(shape),
+                in1=cs[:, :, base + width * variant : base + width * (variant + 1)].unsqueeze(2).broadcast_to(shape),
+                op=ALU.mult,
+            )
+            tables[m, part, variant] = tab
+
+        grouped, xq = {}, {}
+
+        def transpose_x(t):
+            i, j = divmod(t, BLOCK)
+            words = x_sb[i][:, j, :].bitcast(F32)
+            xt = mx_psum.tile([P, PASSES, 2, P], F32, name="xt", tag="mx")
+            for g in range(PASSES):
+                for u in range(2):
+                    nc.tensor.transpose(xt[:, g, u, :], words[:, 256 * g + u : 256 * (g + 1) : 2], ident[:])
+            return xt
+
+        def copy_x(t, xt):
+            i, j = divmod(t, BLOCK)
+            if j == 0:
+                grouped[i] = work.tile([P, PASSES, NTOK, 4], BF16, name="grouped", bufs=2, align_bytes=64)
+            dst = grouped[i][:].rearrange("p g r t -> p g (r t)").bitcast(F32)
+            nc.scalar.copy(
+                out=dst[:, :, 2 * P * j : 2 * P * (j + 1)].rearrange("p g (r u) -> p g r u", u=2),
+                in_=xt[:].rearrange("p g u r -> p g r u"),
+            )
+
+        def quantise(i):
+            codes = work.tile([P, PASSES, NTOK], U32, name="xcodes", align_bytes=64)
+            scales = work.tile([P, PASSES, NTOK], U8, name="xscales", align_bytes=64)
+            nc.vector.quantize_mx(
+                out=codes[:].rearrange("p g r -> p (g r)").bitcast(E5M2X4),
+                scales=scales[:].rearrange("p g r -> p (g r)"),
+                in_=grouped[i][:].rearrange("p g r t -> p (g r t)"),
+            )
+            xq[i] = (codes, scales)
+
+        zt = {}
+
+        def project(group, fill):
+            i, m = divmod(group, 2)
+            codes, scales = xq[i]
+            acc = mx_psum.tile([P, HEADS_PER_FILL, NTOK], F32, name="acc", tag="mx")
+            for a in range(HEADS_PER_FILL):
+                h = HEADS_PER_FILL * fill + a
+                for g in range(PASSES):
+                    nc.tensor.matmul_mx(
+                        out=acc[:, a, :],
+                        lhsT=w_words[m][:, g, 2 * DH * h : 2 * DH * (h + 1)].bitcast(E2M1X4),
+                        lhsT_scale=w_planes[m][:, g, DH * h : DH * (h + 1)],
+                        rhs=codes[:, g, :].bitcast(E5M2X4),
+                        rhs_scale=scales[:, g, :],
+                        start=(g == 0),
+                        stop=(g == PASSES - 1),
+                    )
+            return acc
+
+        def add_bias(group, fill, acc):
+            m = group % 2
+            for a in range(HEADS_PER_FILL):
+                h = HEADS_PER_FILL * fill + a
+                biased = work.tile([P, NTOK], F32, name="biased", bufs=2 * NH + 2)
+                nc.scalar.activation(
+                    out=biased[:], in_=acc[:, a, :], func=ACT.Identity, bias=bias[:, NH * m + h : NH * m + h + 1]
+                )
+                zt[group, h] = biased
+
+        def unit_place(unit):
+            group, j = divmod(unit, BLOCK)
+            i, m = divmod(group, 2)
+            return group, j, BLOCK * i + j, m
+
+        z = {}
+
+        def transpose_z(unit):
+            group, j, t, m = unit_place(unit)
+            for half in range(2):
+                bank = z_psum.tile([P, 4, DH], F32, name="z", tag="z")
+                for a in range(4):
+                    nc.tensor.transpose(bank[:, a, :], zt[group, 4 * half + a][:, P * j : P * (j + 1)], ident[:])
+                z[unit, half] = bank
+
+        def mean_square(unit, half):
+            squares = work.tile([P, 512], BF16, name="squares")
+            acc = half_eps[:, unit, 0:1] if half == 0 else half_b[:, unit : unit + 1]
+            nc.scalar.activation(
+                out=squares[:], in_=z[unit, half][:].rearrange("p a n -> p (a n)"),
+                func=ACT.Square, scale=1.0 / 32.0, accum_out=acc,
+            )
+
+        def add_eps(unit):
+            nc.vector.tensor_reduce(
+                out=half_a[:, unit : unit + 1], in_=half_eps[:, unit, :], axis=mybir.AxisListType.X, op=ALU.add
+            )
+
+        def inverse_rms(unit):
+            nc.scalar.activation(
+                out=rstd[:, unit : unit + 1], in_=half_b[:, unit : unit + 1],
+                func=ACT.Abs_reciprocal_sqrt, bias=half_a[:, unit : unit + 1],
+            )
+
+        terms = {}
+
+        def rope_terms(unit, half, c):
+            group, j, t, m = unit_place(unit)
+            if (unit, c) not in terms:
+                terms[unit, c] = work.tile([P, NH, DH], F32, name="term%d" % c)
+            variants = (t // ROW_GROUPS, t % ROW_GROUPS, 0)
+            for part, (lo, hi) in enumerate(((0, WF), (WF, WF + WH), (WF + WH, DH))):
+                nc.vector.scalar_tensor_tensor(
+                    out=terms[unit, c][:, 4 * half : 4 * half + 4, lo:hi],
+                    in0=z[unit, half][:, :, lo:hi],
+                    scalar=rstd[:, unit : unit + 1],
+                    in1=tables[m, part, variants[part]][:, c, 4 * half : 4 * half + 4, :],
+                    op0=ALU.mult,
+                    op1=ALU.mult,
+                )
+
+        def finish(eng, unit, lo, hi):
+            group, j, t, m = unit_place(unit)
+            width = DH * (hi - lo)
+            result = work.tile([P, width], F32, name="result", bufs=4)
+            pairs = "p h (j e) -> p (h j) e"
+            eng.tensor_tensor(
+                out=result[:].rearrange("p (j e) -> p j e", e=2),
+                in0=terms[unit, 0][:, lo:hi, :].rearrange(pairs, e=2),
+                in1=terms[unit, 1][:, lo:hi, :].rearrange(pairs, e=2)[:, :, ::-1],
+                op=ALU.add,
+            )
+            nc.sync.dma_start(out=outs[m][P * t : P * (t + 1), DH * lo : DH * hi], in_=result[:])
+
+        spread_gain(0)
+        for t in range(BLOCK):
+            copy_x(t, transpose_x(t))
+        spread_gain(1)
+        bias_t = mx_psum.tile([P, P], BF16, name="bias_t", tag="mx")
+        nc.tensor.transpose(bias_t[:], small[:], ident_bf[:])
+        bias = keep.tile([P, 2 * NH], F32, name="bias")
+        nc.scalar.copy(out=bias[:], in_=bias_t[:, 0 : 2 * NH])
+        gain_f = [keep.tile([P, NH, WF], F32, name="gain_f%d" % m) for m in range(2)]
+        for m in range(2):
+            nc.scalar.copy(out=gain_f[m][:], in_=gain[m][:, :, 0:WF])
+        make_table(nc.vector, gain[0], 0, 2, 0)
+        quantise(0)
+        make_table(nc.vector, gain[0], 0, 0, 0)
+        for r in range(ROW_GROUPS):
+            make_table(nc.vector, gain[0], 0, 1, r)
+        make_table(nc.vector, gain[1], 1, 2, 0)
+        make_table(nc.vector, gain[1], 1, 0, 0)
+        for r in range(ROW_GROUPS):
+            make_table(nc.vector, gain[1], 1, 1, r)
+        for f in range(1, FRAMES):
+            for m in range(2):
+                make_table(nc.gpsimd, gain_f[m], m, 0, f)
+        for fill in range(FILLS):
+            add_bias(0, fill, project(0, fill))
+
+        x_at = {}
+        for t in range(BLOCK, TILES):
+            i, j = divmod(t, BLOCK)
+            x_at[2 * BLOCK * (i - 1) + BLOCK - 2 - (BLOCK - 1 - j)] = t
+        for step in sorted(x_at):
+            if step < 0:
+                copy_x(x_at[step], transpose_x(x_at[step]))
+
+        per_step = FILLS // BLOCK
+        for step in range(UNITS + 1):
+            nxt = step // BLOCK + 1
+            fills = [per_step * (step % BLOCK) + a for a in range(per_step)] if nxt < 2 * BLOCKS else []
+            accs = [project(nxt, fill) for fill in fills]
+            xt = transpose_x(x_at[step]) if step in x_at else None
+            if step < UNITS:
+                transpose_z(step)
+            if accs:
+                add_bias(nxt, fills[0], accs[0])
+            elif step < UNITS:
+                mean_square(step, 0)
+            if step > 0:
+                inverse_rms(step - 1)
+            for fill, acc in list(zip(fills, accs))[1:]:
+                add_bias(nxt, fill, acc)
+            if xt is not None:
+                copy_x(x_at[step], xt)
+            if step < UNITS:
+                if accs:
+                    mean_square(step, 0)
+                mean_square(step, 1)
+            if step > 0:
+                rope_terms(step - 1, 0, 0)
+                rope_terms(step - 1, 0, 1)
+                rope_terms(step - 1, 1, 0)
+            if step < UNITS:
+                add_eps(step)
+            if step > 0:
+                rope_terms(step - 1, 1, 1)
+            if xt is not None and x_at[step] % BLOCK == BLOCK - 1:
+                quantise(x_at[step] // BLOCK)
+            if 0 < step < UNITS:
+                finish(nc.gpsimd, step - 1, 0, NH)
+        finish(nc.vector, UNITS - 1, 0, NH // 2)
+        finish(nc.vector, UNITS - 1, NH // 2, NH)

@@ -22,15 +22,16 @@ TILES = L // P
 ROWS_PER_TILE = P // COLS
 ROW_GROUPS = ROWS // ROWS_PER_TILE
 WF, WH, WW = 44, 42, 42
-BLOCK = 2
-NTOK = BLOCK * P
-BLOCKS = TILES // BLOCK
-HEADS_PER_FILL = 512 // NTOK
-FILLS = NH // HEADS_PER_FILL
+BLOCK_TILES = (1, 1, 2, 2, 2, 2, 2, 2, 2)
+BLOCKS = len(BLOCK_TILES)
+BLOCK_START = [sum(BLOCK_TILES[:i]) for i in range(BLOCKS)]
+BLOCK_OF = [i for i in range(BLOCKS) for j in range(BLOCK_TILES[i])]
 UNITS = 2 * TILES
 FREQ_ROW = 32
-ANG_F, ANG_H, ANG_W = 0, FRAMES * WF, FRAMES * WF + ROW_GROUPS * WH
-ANG = ANG_W + WW
+DIRECT_H = 1
+ANG_F, ANG_H, ANG_ALL = 0, WF, WF + DIRECT_H * WH
+ANG_W = ANG_ALL + WF + WH
+ANG = ANG_ALL + DH
 
 FLOPS = 2 * L * D * 2 * D
 
@@ -40,7 +41,8 @@ def tile_causalwanselfattention_pa_kernel(
 ):
     nc = tc.nc
     outs = [o.rearrange("b l h d -> (b l) (h d)") for o in (out_0, out_1)]
-    x_rows = x.rearrange("b (i t p) d -> (b i) p t d", p=P, t=BLOCK)
+    x_tiles = x.rearrange("b (t p) d -> p (b t) d", p=P)
+    x_rows = [x_tiles[:, BLOCK_START[i] : BLOCK_START[i] + BLOCK_TILES[i], :] for i in range(BLOCKS)]
 
     with ExitStack() as ctx:
         keep = ctx.enter_context(tc.tile_pool(name="keep", bufs=1))
@@ -56,7 +58,7 @@ def tile_causalwanselfattention_pa_kernel(
         )
         for row, vec in ((16, gq), (24, gk), (0, bq), (8, bk)):
             nc.sync.dma_start(out=small[row : row + NH, :], in_=vec.rearrange("(h n) -> h n", n=DH))
-        x_sb = [keep.tile([P, BLOCK, D], BF16, name="x%d" % i) for i in range(BLOCKS)]
+        x_sb = [keep.tile([P, BLOCK_TILES[i], D], BF16, name="x%d" % i) for i in range(BLOCKS)]
         nc.sync.dma_start(out=x_sb[0][:], in_=x_rows[0])
         w_words, w_planes = [], []
         for m, (words, scales) in enumerate(((wq_words, wq_scales), (wk_words, wk_scales))):
@@ -71,7 +73,7 @@ def tile_causalwanselfattention_pa_kernel(
             w_words.append(codes)
             w_planes.append(plane)
             nc.sync.dma_start(out=x_sb[1 + m][:], in_=x_rows[1 + m])
-        for i in range(3, BLOCKS):
+        for i in range(3, 4):
             nc.sync.dma_start(out=x_sb[i][:], in_=x_rows[i])
 
         ident_bf = keep.tile([P, P], BF16, name="ident_bf")
@@ -92,9 +94,9 @@ def tile_causalwanselfattention_pa_kernel(
         half_b = keep.tile([P, UNITS], F32, name="half_b")
         half_a = keep.tile([P, UNITS], F32, name="half_a")
         rstd = keep.tile([P, UNITS], F32, name="rstd")
-        sel_h = keep.tile([P, ROWS, COLS], BF16, name="sel_h")
+        sel_h = keep.tile([P, DIRECT_H * ROWS_PER_TILE, COLS], BF16, name="sel_h")
         nc.vector.tensor_copy(
-            out=sel_h[:], in_=ident_bf[:, FREQ_ROW : FREQ_ROW + ROWS].unsqueeze(2).broadcast_to([P, ROWS, COLS])
+            out=sel_h[:], in_=ident_bf[:, FREQ_ROW : FREQ_ROW + DIRECT_H * ROWS_PER_TILE].unsqueeze(2).broadcast_to([P, DIRECT_H * ROWS_PER_TILE, COLS])
         )
         sel_w = keep.tile([P, ROWS_PER_TILE, COLS], BF16, name="sel_w")
         nc.vector.tensor_copy(
@@ -106,20 +108,18 @@ def tile_causalwanselfattention_pa_kernel(
             return ident_bf[:, row : row + 1].to_broadcast([P, P])
 
         ang = mx_psum.tile([P, 512], F32, name="ang", tag="mx")
-        for f in range(FRAMES):
-            nc.tensor.matmul(
-                out=ang[:, ANG_F + WF * f : ANG_F + WF * (f + 1)], lhsT=row_to_all(FREQ_ROW + f),
-                rhs=small[:, 0:WF], start=True, stop=True,
-            )
-        for r in range(ROW_GROUPS):
+        nc.tensor.matmul(
+            out=ang[:, ANG_F : ANG_F + WF], lhsT=row_to_all(FREQ_ROW), rhs=small[:, 0:WF], start=True, stop=True
+        )
+        for r in range(DIRECT_H):
             nc.tensor.matmul(
                 out=ang[:, ANG_H + WH * r : ANG_H + WH * (r + 1)],
                 lhsT=sel_h[:, ROWS_PER_TILE * r : ROWS_PER_TILE * (r + 1), :].rearrange("p a b -> p (a b)"),
                 rhs=small[:, WF : WF + WH], start=True, stop=True,
             )
         nc.tensor.matmul(
-            out=ang[:, ANG_W:ANG], lhsT=sel_w[:].rearrange("p a b -> p (a b)"),
-            rhs=small[:, WF + WH : DH], start=True, stop=True,
+            out=ang[:, ANG_ALL:ANG], lhsT=sel_w[:].rearrange("p a b -> p (a b)"),
+            rhs=small[:], start=True, stop=True,
         )
         cs = keep.tile([P, 2, ANG], F32, name="cs")
         shape = [P, 2, ANG // 2, 2]
@@ -157,7 +157,8 @@ def tile_causalwanselfattention_pa_kernel(
         grouped, xq = {}, {}
 
         def transpose_x(t):
-            i, j = divmod(t, BLOCK)
+            i = BLOCK_OF[t]
+            j = t - BLOCK_START[i]
             words = x_sb[i][:, j, :].bitcast(F32)
             xt = mx_psum.tile([P, PASSES, 2, P], F32, name="xt", tag="mx")
             for g in range(PASSES):
@@ -165,19 +166,20 @@ def tile_causalwanselfattention_pa_kernel(
                     nc.tensor.transpose(xt[:, g, u, :], words[:, 256 * g + u : 256 * (g + 1) : 2], ident[:])
             return xt
 
-        def copy_x(t, xt):
-            i, j = divmod(t, BLOCK)
-            if j == 0:
-                grouped[i] = work.tile([P, PASSES, NTOK, 4], BF16, name="grouped", bufs=2, align_bytes=64)
+        def copy_x(t, xt, copy=nc.scalar.copy, passes=slice(0, PASSES)):
+            i = BLOCK_OF[t]
+            j = t - BLOCK_START[i]
+            if i not in grouped:
+                grouped[i] = work.tile([P, PASSES, P * BLOCK_TILES[i], 4], BF16, name="grouped", bufs=2, align_bytes=64)
             dst = grouped[i][:].rearrange("p g r t -> p g (r t)").bitcast(F32)
-            nc.scalar.copy(
-                out=dst[:, :, 2 * P * j : 2 * P * (j + 1)].rearrange("p g (r u) -> p g r u", u=2),
-                in_=xt[:].rearrange("p g u r -> p g r u"),
+            copy(
+                out=dst[:, passes, 2 * P * j : 2 * P * (j + 1)].rearrange("p g (r u) -> p g r u", u=2),
+                in_=xt[:, passes].rearrange("p g u r -> p g r u"),
             )
 
         def quantise(i):
-            codes = work.tile([P, PASSES, NTOK], U32, name="xcodes", align_bytes=64)
-            scales = work.tile([P, PASSES, NTOK], U8, name="xscales", align_bytes=64)
+            codes = work.tile([P, PASSES, P * BLOCK_TILES[i]], U32, name="xcodes", align_bytes=64)
+            scales = work.tile([P, PASSES, P * BLOCK_TILES[i]], U8, name="xscales", align_bytes=64)
             nc.vector.quantize_mx(
                 out=codes[:].rearrange("p g r -> p (g r)").bitcast(E5M2X4),
                 scales=scales[:].rearrange("p g r -> p (g r)"),
@@ -190,9 +192,10 @@ def tile_causalwanselfattention_pa_kernel(
         def project(group, fill):
             i, m = divmod(group, 2)
             codes, scales = xq[i]
-            acc = mx_psum.tile([P, HEADS_PER_FILL, NTOK], F32, name="acc", tag="mx")
-            for a in range(HEADS_PER_FILL):
-                h = HEADS_PER_FILL * fill + a
+            heads = 4 // BLOCK_TILES[i]
+            acc = mx_psum.tile([P, heads, P * BLOCK_TILES[i]], F32, name="acc", tag="mx")
+            for a in range(heads):
+                h = heads * fill + a
                 for g in range(PASSES):
                     nc.tensor.matmul_mx(
                         out=acc[:, a, :],
@@ -206,19 +209,20 @@ def tile_causalwanselfattention_pa_kernel(
             return acc
 
         def add_bias(group, fill, acc):
-            m = group % 2
-            for a in range(HEADS_PER_FILL):
-                h = HEADS_PER_FILL * fill + a
-                biased = work.tile([P, NTOK], F32, name="biased", bufs=2 * NH + 2)
+            i, m = divmod(group, 2)
+            heads = 4 // BLOCK_TILES[i]
+            for a in range(heads):
+                h = heads * fill + a
+                biased = work.tile([P, P * BLOCK_TILES[i]], F32, name="biased", bufs=2 * NH + 2)
                 nc.scalar.activation(
                     out=biased[:], in_=acc[:, a, :], func=ACT.Identity, bias=bias[:, NH * m + h : NH * m + h + 1]
                 )
                 zt[group, h] = biased
 
         def unit_place(unit):
-            group, j = divmod(unit, BLOCK)
-            i, m = divmod(group, 2)
-            return group, j, BLOCK * i + j, m
+            i = BLOCK_OF[unit // 2]
+            m, j = divmod(unit - 2 * BLOCK_START[i], BLOCK_TILES[i])
+            return 2 * i + m, j, BLOCK_START[i] + j, m
 
         z = {}
 
@@ -254,7 +258,7 @@ def tile_causalwanselfattention_pa_kernel(
         def rope_terms(unit, half, c):
             group, j, t, m = unit_place(unit)
             if (unit, c) not in terms:
-                terms[unit, c] = work.tile([P, NH, DH], F32, name="term%d" % c)
+                terms[unit, c] = work.tile([P, NH, DH], F32, name="term%d" % c, bufs=4)
             variants = (t // ROW_GROUPS, t % ROW_GROUPS, 0)
             for part, (lo, hi) in enumerate(((0, WF), (WF, WF + WH), (WF + WH, DH))):
                 nc.vector.scalar_tensor_tensor(
@@ -269,7 +273,7 @@ def tile_causalwanselfattention_pa_kernel(
         def finish(eng, unit, lo, hi):
             group, j, t, m = unit_place(unit)
             width = DH * (hi - lo)
-            result = work.tile([P, width], F32, name="result", bufs=4)
+            result = work.tile([P, width], F32, name="result", bufs=5)
             pairs = "p h (j e) -> p (h j) e"
             eng.tensor_tensor(
                 out=result[:].rearrange("p (j e) -> p j e", e=2),
@@ -279,73 +283,123 @@ def tile_causalwanselfattention_pa_kernel(
             )
             nc.sync.dma_start(out=outs[m][P * t : P * (t + 1), DH * lo : DH * hi], in_=result[:])
 
-        spread_gain(0)
-        for t in range(BLOCK):
-            copy_x(t, transpose_x(t))
-        spread_gain(1)
         bias_t = mx_psum.tile([P, P], BF16, name="bias_t", tag="mx")
-        nc.tensor.transpose(bias_t[:], small[:], ident_bf[:])
         bias = keep.tile([P, 2 * NH], F32, name="bias")
+        gain_sb = [keep.tile([COLS, NH, WF + WH], BF16, name="gain_sb%d" % m) for m in range(2)]
+        first = BLOCK_TILES[0]
+        nc.tensor.transpose(bias_t[:], small[:], ident_bf[:])
         nc.scalar.copy(out=bias[:], in_=bias_t[:, 0 : 2 * NH])
-        gain_f = [keep.tile([P, NH, WF], F32, name="gain_f%d" % m) for m in range(2)]
-        for m in range(2):
-            nc.scalar.copy(out=gain_f[m][:], in_=gain[m][:, :, 0:WF])
-        make_table(nc.vector, gain[0], 0, 2, 0)
+        for t in range(first):
+            copy_x(t, transpose_x(t))
         quantise(0)
-        make_table(nc.vector, gain[0], 0, 0, 0)
-        for r in range(ROW_GROUPS):
-            make_table(nc.vector, gain[0], 0, 1, r)
-        make_table(nc.vector, gain[1], 1, 2, 0)
-        make_table(nc.vector, gain[1], 1, 0, 0)
-        for r in range(ROW_GROUPS):
-            make_table(nc.vector, gain[1], 1, 1, r)
-        for f in range(1, FRAMES):
-            for m in range(2):
-                make_table(nc.gpsimd, gain_f[m], m, 0, f)
-        for fill in range(FILLS):
+        spread_gain(0)
+        for fill in range(2 * first):
             add_bias(0, fill, project(0, fill))
+        spread_gain(1)
+        copy_x(first, transpose_x(first))
 
-        x_at = {}
-        for t in range(BLOCK, TILES):
-            i, j = divmod(t, BLOCK)
-            x_at[2 * BLOCK * (i - 1) + BLOCK - 2 - (BLOCK - 1 - j)] = t
-        for step in sorted(x_at):
-            if step < 0:
-                copy_x(x_at[step], transpose_x(x_at[step]))
+        park = outs[1][L - P : L, :].rearrange("r d -> (r d)")
+        parked = {}
 
-        per_step = FILLS // BLOCK
+        def park_rows(m, part):
+            rows, col, width, lo = ((FRAMES, 0, WF, 1), (ROWS, WF, WH, ROWS_PER_TILE * DIRECT_H))[part]
+            by_row = keep.tile([COLS, 2, NH, width], F32, name="by_row%d_%d" % (m, part))
+            shape = [COLS, 2, NH, width]
+            nc.gpsimd.tensor_tensor(
+                out=by_row[:],
+                in0=gain_sb[m][:, :, col : col + width].unsqueeze(1).broadcast_to(shape),
+                in1=cs[0:COLS, :, ANG_ALL + col : ANG_ALL + col + width].unsqueeze(2).broadcast_to(shape),
+                op=ALU.mult,
+            )
+            size = 2 * NH * width
+            offset = (2 * part + m) * ROWS * 2 * NH * WF
+            parked[m, part] = park[offset : offset + rows * size].rearrange("(r n) -> r n", n=size)
+            nc.sync.dma_start(out=parked[m, part][lo:rows, :], in_=by_row[lo:rows].rearrange("p c h n -> p (c h n)"))
+
+        def spread_row_tables(m):
+            tabs = keep.tile([P, ROW_GROUPS - DIRECT_H, 2, NH, WH], F32, name="row_tabs%d" % m)
+            for r in range(ROWS_PER_TILE):
+                nc.sync.dma_start(
+                    out=tabs[COLS * r : COLS * (r + 1)].rearrange("p v c h n -> p v (c h n)"),
+                    in_=parked[m, 1][ROWS_PER_TILE * DIRECT_H + r : ROWS : ROWS_PER_TILE, :].partition_broadcast(COLS),
+                )
+            for v in range(DIRECT_H, ROW_GROUPS):
+                tables[m, 1, v] = tabs[:, v - DIRECT_H]
+
+        def spread_frame_table(m, f):
+            tab = keep.tile([P, 2, NH, WF], F32, name="frame_tab%d_%d" % (m, f))
+            nc.sync.dma_start(
+                out=tab[:].rearrange("p c h n -> p (c h n)"), in_=parked[m, 0][f, :].partition_broadcast(P)
+            )
+            tables[m, 0, f] = tab
+
+        for m in range(2):
+            nc.vector.tensor_copy(out=gain_sb[m][:], in_=gain[m][0:COLS, :, 0 : WF + WH])
+            if m == 1 and first == 1:
+                quantise(1)
+            for part, variant in [(2, 0), (0, 0)] + [(1, r) for r in range(DIRECT_H)]:
+                make_table(nc.vector, gain[m], m, part, variant)
+            park_rows(m, 1)
+        for m in range(2):
+            spread_row_tables(m)
+        for m in range(2):
+            park_rows(m, 0)
+        for i in range(4, BLOCKS):
+            nc.sync.dma_start(out=x_sb[i][:], in_=x_rows[i])
+
+        x_at, quantise_at = {}, {}
+        for i in range(1, BLOCKS):
+            first_fill = 2 * BLOCK_START[i] - BLOCK_TILES[i - 1]
+            for j in range(BLOCK_TILES[i]):
+                x_at[first_fill - 1 - BLOCK_TILES[i] + j] = BLOCK_START[i] + j
+            quantise_at[first_fill - 2] = i
+
         for step in range(UNITS + 1):
-            nxt = step // BLOCK + 1
-            fills = [per_step * (step % BLOCK) + a for a in range(per_step)] if nxt < 2 * BLOCKS else []
-            accs = [project(nxt, fill) for fill in fills]
+            fills = []
+            if step < UNITS:
+                group, j, t, m = unit_place(step)
+                nxt = group + 1
+                if nxt < 2 * BLOCKS:
+                    count, steps = 2 * BLOCK_TILES[nxt // 2], BLOCK_TILES[group // 2]
+                    fills = list(range(count * j // steps, count * (j + 1) // steps))
+            accs = [project(nxt, fill) for fill in fills[:2]]
             xt = transpose_x(x_at[step]) if step in x_at else None
             if step < UNITS:
                 transpose_z(step)
-            if accs:
+            on_vector = xt is not None and x_at[step] in (4, 6, 8, 10, 12, 14)
+            if fills:
                 add_bias(nxt, fills[0], accs[0])
             elif step < UNITS:
                 mean_square(step, 0)
+
             if step > 0:
                 inverse_rms(step - 1)
-            for fill, acc in list(zip(fills, accs))[1:]:
-                add_bias(nxt, fill, acc)
+            if len(fills) > 1:
+                add_bias(nxt, fills[1], accs[1])
             if xt is not None:
-                copy_x(x_at[step], xt)
+                copy_x(x_at[step], xt, passes=slice(0, 1 if on_vector else PASSES))
             if step < UNITS:
-                if accs:
+                if fills:
                     mean_square(step, 0)
                 mean_square(step, 1)
+            for fill in fills[2:]:
+                add_bias(nxt, fill, project(nxt, fill))
             if step > 0:
                 rope_terms(step - 1, 0, 0)
                 rope_terms(step - 1, 0, 1)
+            if on_vector:
+                copy_x(x_at[step], xt, nc.vector.tensor_copy, slice(1, PASSES))
+            if step > 0:
                 rope_terms(step - 1, 1, 0)
             if step < UNITS:
                 add_eps(step)
             if step > 0:
                 rope_terms(step - 1, 1, 1)
-            if xt is not None and x_at[step] % BLOCK == BLOCK - 1:
-                quantise(x_at[step] // BLOCK)
+            if step in quantise_at:
+                quantise(quantise_at[step])
             if 0 < step < UNITS:
                 finish(nc.gpsimd, step - 1, 0, NH)
+            if 1 <= step < 1 + 2 * (FRAMES - 1):
+                spread_frame_table((step - 1) % 2, 1 + (step - 1) // 2)
         finish(nc.vector, UNITS - 1, 0, NH // 2)
         finish(nc.vector, UNITS - 1, NH // 2, NH)

@@ -28,7 +28,7 @@ BLOCK_START = [sum(BLOCK_TILES[:i]) for i in range(BLOCKS)]
 BLOCK_OF = [i for i in range(BLOCKS) for j in range(BLOCK_TILES[i])]
 UNITS = 2 * TILES
 FREQ_ROW = 32
-DIRECT_H = 1
+DIRECT_H = 2
 ANG_F, ANG_H, ANG_ALL = 0, WF, WF + DIRECT_H * WH
 ANG_W = ANG_ALL + WF + WH
 ANG = ANG_ALL + DH
@@ -83,16 +83,8 @@ def tile_causalwanselfattention_pa_kernel(
         sign = keep.tile([P, 2, 2], F32, name="sign")
         nc.vector.memset(sign[:], 1.0)
         nc.vector.memset(sign[:, 1, 1:2], -1.0)
-        half_eps = keep.tile([P, UNITS, 2], F32, name="half_eps")
-        nc.vector.tensor_scalar(
-            out=half_eps[:, :, 1:2],
-            in0=sign[:, 0, 0:1].unsqueeze(1).broadcast_to([P, UNITS, 1]),
-            scalar1=EPS,
-            scalar2=None,
-            op0=ALU.mult,
-        )
-        half_b = keep.tile([P, UNITS], F32, name="half_b")
-        half_a = keep.tile([P, UNITS], F32, name="half_a")
+        half_sq = keep.tile([P, UNITS, 2], F32, name="half_sq")
+        mean_sq = keep.tile([P, UNITS], F32, name="mean_sq")
         rstd = keep.tile([P, UNITS], F32, name="rstd")
         sel_h = keep.tile([P, DIRECT_H * ROWS_PER_TILE, COLS], BF16, name="sel_h")
         nc.vector.tensor_copy(
@@ -208,10 +200,10 @@ def tile_causalwanselfattention_pa_kernel(
                     )
             return acc
 
-        def add_bias(group, fill, acc):
+        def add_bias(group, fill, acc, part=None):
             i, m = divmod(group, 2)
             heads = 4 // BLOCK_TILES[i]
-            for a in range(heads):
+            for a in range(heads)[part or slice(None)]:
                 h = heads * fill + a
                 biased = work.tile([P, P * BLOCK_TILES[i]], F32, name="biased", bufs=2 * NH + 2)
                 nc.scalar.activation(
@@ -236,21 +228,22 @@ def tile_causalwanselfattention_pa_kernel(
 
         def mean_square(unit, half):
             squares = work.tile([P, 512], BF16, name="squares")
-            acc = half_eps[:, unit, 0:1] if half == 0 else half_b[:, unit : unit + 1]
+            acc = half_sq[:, unit, half : half + 1]
             nc.scalar.activation(
                 out=squares[:], in_=z[unit, half][:].rearrange("p a n -> p (a n)"),
                 func=ACT.Square, scale=1.0 / 32.0, accum_out=acc,
             )
 
-        def add_eps(unit):
-            nc.vector.tensor_reduce(
-                out=half_a[:, unit : unit + 1], in_=half_eps[:, unit, :], axis=mybir.AxisListType.X, op=ALU.add
+        def add_halves(unit):
+            nc.scalar.activation(
+                out=mean_sq[:, unit : unit + 1], in_=half_sq[:, unit, 0:1],
+                func=ACT.Identity, bias=half_sq[:, unit, 1:2],
             )
 
         def inverse_rms(unit):
             nc.scalar.activation(
-                out=rstd[:, unit : unit + 1], in_=half_b[:, unit : unit + 1],
-                func=ACT.Abs_reciprocal_sqrt, bias=half_a[:, unit : unit + 1],
+                out=rstd[:, unit : unit + 1], in_=mean_sq[:, unit : unit + 1],
+                func=ACT.Abs_reciprocal_sqrt, bias=EPS,
             )
 
         terms = {}
@@ -366,12 +359,15 @@ def tile_causalwanselfattention_pa_kernel(
             xt = transpose_x(x_at[step]) if step in x_at else None
             if step < UNITS:
                 transpose_z(step)
-            on_vector = xt is not None and x_at[step] in (4, 6, 8, 10, 12, 14)
+            on_vector = xt is not None and x_at[step] in range(2, 16)
             if fills:
-                add_bias(nxt, fills[0], accs[0])
+                add_bias(nxt, fills[0], accs[0], slice(0, 1))
             elif step < UNITS:
                 mean_square(step, 0)
-
+            if step > 0:
+                add_halves(step - 1)
+            if fills:
+                add_bias(nxt, fills[0], accs[0], slice(1, None))
             if step > 0:
                 inverse_rms(step - 1)
             if len(fills) > 1:
@@ -391,8 +387,7 @@ def tile_causalwanselfattention_pa_kernel(
                 copy_x(x_at[step], xt, nc.vector.tensor_copy, slice(1, PASSES))
             if step > 0:
                 rope_terms(step - 1, 1, 0)
-            if step < UNITS:
-                add_eps(step)
+
             if step > 0:
                 rope_terms(step - 1, 1, 1)
             if step in quantise_at:

@@ -83,6 +83,8 @@ def tile_causalwanselfattention_pa_kernel(
         sign = keep.tile([P, 2, 2], F32, name="sign")
         nc.vector.memset(sign[:], 1.0)
         nc.vector.memset(sign[:, 1, 1:2], -1.0)
+        warm = keep.tile([P, 1], F32, name="warm")
+        nc.scalar.activation(out=warm[:], in_=sign[:, 0, 0:1], func=ACT.Abs_reciprocal_sqrt)
         half_sq = keep.tile([P, UNITS, 2], F32, name="half_sq")
         mean_sq = keep.tile([P, UNITS], F32, name="mean_sq")
         rstd = keep.tile([P, UNITS], F32, name="rstd")

from contextlib import ExitStack

import concourse.mybir as mybir
from concourse.masks import make_identity

F32 = mybir.dt.float32
BF16 = mybir.dt.bfloat16
I32 = mybir.dt.int32
U32 = mybir.dt.uint32
U8 = mybir.dt.uint8
E5M2X4 = mybir.dt.float8_e5m2_x4
E2M1X4 = mybir.dt.float4_e2m1fn_x4
ACT = mybir.ActivationFunctionType
ALU = mybir.AluOpType

P = 128
L, D, NH, DH = 2048, 1024, 8, 128
FRAMES, ROWS, COLS = 4, 16, 32
EPS = 1.0e-6
PASSES = D // 512
TILES = L // P
ROWS_PER_TILE = P // COLS
ROW_GROUPS = ROWS // ROWS_PER_TILE
WF, WH, WW = 44, 42, 42
BLOCK_TILES = (1, 1, 2, 2, 2, 2, 2, 2, 2)
BLOCKS = len(BLOCK_TILES)
BLOCK_START = [sum(BLOCK_TILES[:i]) for i in range(BLOCKS)]
BLOCK_OF = [i for i in range(BLOCKS) for j in range(BLOCK_TILES[i])]
UNITS = 2 * TILES
FREQ_ROW = 32
DIRECT_H = 2
ANG_F, ANG_H, ANG_ALL = 0, WF, WF + DIRECT_H * WH
ANG_W = ANG_ALL + WF + WH
ANG = ANG_ALL + DH

FLOPS = 2 * L * D * 2 * D


def tile_causalwanselfattention_pa_kernel(
    tc, x, wq_words, wq_scales, bq, wk_words, wk_scales, bk, gq, gk, freqs, out_0, out_1
):
    nc = tc.nc
    outs = [o.rearrange("b l h d -> (b l) (h d)") for o in (out_0, out_1)]
    x_tiles = x.rearrange("b (t p) d -> p (b t) d", p=P)
    x_rows = [x_tiles[:, BLOCK_START[i] : BLOCK_START[i] + BLOCK_TILES[i], :] for i in range(BLOCKS)]

    with ExitStack() as ctx:
        keep = ctx.enter_context(tc.tile_pool(name="keep", bufs=1))
        work = ctx.enter_context(tc.tile_pool(name="work", bufs=3))
        mx_psum = ctx.enter_context(tc.psum_pool(name="mx_psum", bufs=3))
        z_psum = ctx.enter_context(tc.psum_pool(name="z_psum", bufs=5))
        ctx.enter_context(tc.manual_schedule())

        small = keep.tile([P, DH], BF16, name="small")
        nc.vector.memset(small[64:P, :], 0.0)
        nc.sync.dma_start(
            out=small[FREQ_ROW : FREQ_ROW + COLS, :], in_=freqs[0:COLS].rearrange("r j c -> r (j c)")
        )
        for row, vec in ((16, gq), (24, gk), (0, bq), (8, bk)):
            nc.sync.dma_start(out=small[row : row + NH, :], in_=vec.rearrange("(h n) -> h n", n=DH))
        x_sb = [keep.tile([P, BLOCK_TILES[i], D], BF16, name="x%d" % i) for i in range(BLOCKS)]
        nc.sync.dma_start(out=x_sb[0][:], in_=x_rows[0])
        w_words, w_planes = [], []
        for m, (words, scales) in enumerate(((wq_words, wq_scales), (wk_words, wk_scales))):
            plane = keep.tile([P, PASSES, D], U8, name="plane%d" % m, align_bytes=64)
            for quad in range(4):
                nc.sync.dma_start(
                    out=plane[32 * quad : 32 * quad + 4, :, :].bitcast(I32),
                    in_=scales[:, 4 * quad : 4 * quad + 4, :].rearrange("g r n -> r g n").bitcast(I32),
                )
            codes = keep.tile([P, PASSES, 2 * D], U8, name="words%d" % m, align_bytes=64)
            nc.sync.dma_start(out=codes[:].bitcast(I32), in_=words.rearrange("g p n -> p g n").bitcast(I32))
            w_words.append(codes)
            w_planes.append(plane)
            nc.sync.dma_start(out=x_sb[1 + m][:], in_=x_rows[1 + m])
        for i in range(3, 4):
            nc.sync.dma_start(out=x_sb[i][:], in_=x_rows[i])

        ident_bf = keep.tile([P, P], BF16, name="ident_bf")
        make_identity(nc, ident_bf[:])
        ident = keep.tile([P, P], F32, name="ident")
        make_identity(nc, ident[:])
        sign = keep.tile([P, 2, 2], F32, name="sign")
        nc.vector.memset(sign[:], 1.0)
        nc.vector.memset(sign[:, 1, 1:2], -1.0)
        warm = keep.tile([P, 1], F32, name="warm")
        nc.scalar.activation(out=warm[:], in_=sign[:, 0, 0:1], func=ACT.Abs_reciprocal_sqrt)
        half_sq = keep.tile([P, UNITS, 2], F32, name="half_sq")
        mean_sq = keep.tile([P, UNITS], F32, name="mean_sq")
        rstd = keep.tile([P, UNITS], F32, name="rstd")
        sel_h = keep.tile([P, DIRECT_H * ROWS_PER_TILE, COLS], BF16, name="sel_h")
        nc.vector.tensor_copy(
            out=sel_h[:], in_=ident_bf[:, FREQ_ROW : FREQ_ROW + DIRECT_H * ROWS_PER_TILE].unsqueeze(2).broadcast_to([P, DIRECT_H * ROWS_PER_TILE, COLS])
        )
        sel_w = keep.tile([P, ROWS_PER_TILE, COLS], BF16, name="sel_w")
        nc.vector.tensor_copy(
            out=sel_w[:],
            in_=ident_bf[:, FREQ_ROW : FREQ_ROW + COLS].unsqueeze(1).broadcast_to([P, ROWS_PER_TILE, COLS]),
        )

        def row_to_all(row):
            return ident_bf[:, row : row + 1].to_broadcast([P, P])

        ang = mx_psum.tile([P, 512], F32, name="ang", tag="mx")
        nc.tensor.matmul(
            out=ang[:, ANG_F : ANG_F + WF], lhsT=row_to_all(FREQ_ROW), rhs=small[:, 0:WF], start=True, stop=True
        )
        for r in range(DIRECT_H):
            nc.tensor.matmul(
                out=ang[:, ANG_H + WH * r : ANG_H + WH * (r + 1)],
                lhsT=sel_h[:, ROWS_PER_TILE * r : ROWS_PER_TILE * (r + 1), :].rearrange("p a b -> p (a b)"),
                rhs=small[:, WF : WF + WH], start=True, stop=True,
            )
        nc.tensor.matmul(
            out=ang[:, ANG_ALL:ANG], lhsT=sel_w[:].rearrange("p a b -> p (a b)"),
            rhs=small[:], start=True, stop=True,
        )
        cs = keep.tile([P, 2, ANG], F32, name="cs")
        shape = [P, 2, ANG // 2, 2]
        nc.vector.tensor_tensor(
            out=cs[:].rearrange("p c (j e) -> p c j e", e=2),
            in0=ang[:, 0:ANG].rearrange("p (j c) -> p c j", c=2).unsqueeze(3).broadcast_to(shape),
            in1=sign[:].unsqueeze(2).broadcast_to(shape),
            op=ALU.mult,
        )

        gain = []

        def spread_gain(m):
            bank = z_psum.tile([P, NH, DH], BF16, name="gain%d" % m, tag="z")
            for h in range(NH):
                nc.tensor.matmul(
                    out=bank[:, h, :], lhsT=row_to_all(16 + NH * m + h), rhs=small[:], start=True, stop=True
                )
            gain.append(bank)

        tables = {}

        def make_table(eng, gsrc, m, part, variant):
            col, width, base = ((0, WF, ANG_F), (WF, WH, ANG_H), (WF + WH, WW, ANG_W))[part]
            tab = keep.tile([P, 2, NH, width], F32, name="tab%d_%d_%d" % (m, part, variant))
            shape = [P, 2, NH, width]
            eng.tensor_tensor(
                out=tab[:],
                in0=gsrc[:, :, col : col + width].unsqueeze(1).broadcast_to(shape),
                in1=cs[:, :, base + width * variant : base + width * (variant + 1)].unsqueeze(2).broadcast_to(shape),
                op=ALU.mult,
            )
            tables[m, part, variant] = tab

        grouped, xq = {}, {}

        def transpose_x(t):
            i = BLOCK_OF[t]
            j = t - BLOCK_START[i]
            words = x_sb[i][:, j, :].bitcast(F32)
            xt = mx_psum.tile([P, PASSES, 2, P], F32, name="xt", tag="mx")
            for g in range(PASSES):
                for u in range(2):
                    nc.tensor.transpose(xt[:, g, u, :], words[:, 256 * g + u : 256 * (g + 1) : 2], ident[:])
            return xt

        def copy_x(t, xt, copy=nc.scalar.copy, passes=slice(0, PASSES)):
            i = BLOCK_OF[t]
            j = t - BLOCK_START[i]
            if i not in grouped:
                grouped[i] = work.tile([P, PASSES, P * BLOCK_TILES[i], 4], BF16, name="grouped", bufs=2, align_bytes=64)
            dst = grouped[i][:].rearrange("p g r t -> p g (r t)").bitcast(F32)
            copy(
                out=dst[:, passes, 2 * P * j : 2 * P * (j + 1)].rearrange("p g (r u) -> p g r u", u=2),
                in_=xt[:, passes].rearrange("p g u r -> p g r u"),
            )

        def quantise(i):
            codes = work.tile([P, PASSES, P * BLOCK_TILES[i]], U32, name="xcodes", align_bytes=64)
            scales = work.tile([P, PASSES, P * BLOCK_TILES[i]], U8, name="xscales", align_bytes=64)
            nc.vector.quantize_mx(
                out=codes[:].rearrange("p g r -> p (g r)").bitcast(E5M2X4),
                scales=scales[:].rearrange("p g r -> p (g r)"),
                in_=grouped[i][:].rearrange("p g r t -> p (g r t)"),
            )
            xq[i] = (codes, scales)

        zt = {}

        def project(group, fill):
            i, m = divmod(group, 2)
            codes, scales = xq[i]
            heads = 4 // BLOCK_TILES[i]
            acc = mx_psum.tile([P, heads, P * BLOCK_TILES[i]], F32, name="acc", tag="mx")
            for a in range(heads):
                h = heads * fill + a
                for g in range(PASSES):
                    nc.tensor.matmul_mx(
                        out=acc[:, a, :],
                        lhsT=w_words[m][:, g, 2 * DH * h : 2 * DH * (h + 1)].bitcast(E2M1X4),
                        lhsT_scale=w_planes[m][:, g, DH * h : DH * (h + 1)],
                        rhs=codes[:, g, :].bitcast(E5M2X4),
                        rhs_scale=scales[:, g, :],
                        start=(g == 0),
                        stop=(g == PASSES - 1),
                    )
            return acc

        def add_bias(group, fill, acc, part=None):
            i, m = divmod(group, 2)
            heads = 4 // BLOCK_TILES[i]
            for a in range(heads)[part or slice(None)]:
                h = heads * fill + a
                biased = work.tile([P, P * BLOCK_TILES[i]], F32, name="biased", bufs=2 * NH + 2)
                nc.scalar.activation(
                    out=biased[:], in_=acc[:, a, :], func=ACT.Identity, bias=bias[:, NH * m + h : NH * m + h + 1]
                )
                zt[group, h] = biased

        def unit_place(unit):
            i = BLOCK_OF[unit // 2]
            m, j = divmod(unit - 2 * BLOCK_START[i], BLOCK_TILES[i])
            return 2 * i + m, j, BLOCK_START[i] + j, m

        z = {}

        def transpose_z(unit):
            group, j, t, m = unit_place(unit)
            for half in range(2):
                bank = z_psum.tile([P, 4, DH], F32, name="z", tag="z")
                for a in range(4):
                    nc.tensor.transpose(bank[:, a, :], zt[group, 4 * half + a][:, P * j : P * (j + 1)], ident[:])
                z[unit, half] = bank

        def mean_square(unit, half):
            squares = work.tile([P, 512], BF16, name="squares")
            acc = half_sq[:, unit, half : half + 1]
            nc.scalar.activation(
                out=squares[:], in_=z[unit, half][:].rearrange("p a n -> p (a n)"),
                func=ACT.Square, scale=1.0 / 32.0, accum_out=acc,
            )

        def add_halves(unit):
            nc.scalar.activation(
                out=mean_sq[:, unit : unit + 1], in_=half_sq[:, unit, 0:1],
                func=ACT.Identity, bias=half_sq[:, unit, 1:2],
            )

        def inverse_rms(unit):
            nc.scalar.activation(
                out=rstd[:, unit : unit + 1], in_=mean_sq[:, unit : unit + 1],
                func=ACT.Abs_reciprocal_sqrt, bias=EPS,
            )

        terms = {}

        def rope_terms(unit, half, c):
            group, j, t, m = unit_place(unit)
            if (unit, c) not in terms:
                terms[unit, c] = work.tile([P, NH, DH], F32, name="term%d" % c, bufs=4)
            variants = (t // ROW_GROUPS, t % ROW_GROUPS, 0)
            for part, (lo, hi) in enumerate(((0, WF), (WF, WF + WH), (WF + WH, DH))):
                nc.vector.scalar_tensor_tensor(
                    out=terms[unit, c][:, 4 * half : 4 * half + 4, lo:hi],
                    in0=z[unit, half][:, :, lo:hi],
                    scalar=rstd[:, unit : unit + 1],
                    in1=tables[m, part, variants[part]][:, c, 4 * half : 4 * half + 4, :],
                    op0=ALU.mult,
                    op1=ALU.mult,
                )

        def finish(eng, unit, lo, hi):
            group, j, t, m = unit_place(unit)
            width = DH * (hi - lo)
            result = work.tile([P, width], F32, name="result", bufs=5)
            pairs = "p h (j e) -> p (h j) e"
            eng.tensor_tensor(
                out=result[:].rearrange("p (j e) -> p j e", e=2),
                in0=terms[unit, 0][:, lo:hi, :].rearrange(pairs, e=2),
                in1=terms[unit, 1][:, lo:hi, :].rearrange(pairs, e=2)[:, :, ::-1],
                op=ALU.add,
            )
            nc.sync.dma_start(out=outs[m][P * t : P * (t + 1), DH * lo : DH * hi], in_=result[:])

        bias_t = mx_psum.tile([P, P], BF16, name="bias_t", tag="mx")
        bias = keep.tile([P, 2 * NH], F32, name="bias")
        gain_sb = [keep.tile([COLS, NH, WF + WH], BF16, name="gain_sb%d" % m) for m in range(2)]
        first = BLOCK_TILES[0]
        nc.tensor.transpose(bias_t[:], small[:], ident_bf[:])
        nc.scalar.copy(out=bias[:], in_=bias_t[:, 0 : 2 * NH])
        for t in range(first):
            copy_x(t, transpose_x(t))
        quantise(0)
        spread_gain(0)
        for fill in range(2 * first):
            add_bias(0, fill, project(0, fill))
        spread_gain(1)
        copy_x(first, transpose_x(first))

        park = outs[1][L - P : L, :].rearrange("r d -> (r d)")
        parked = {}

        def park_rows(m, part):
            rows, col, width, lo = ((FRAMES, 0, WF, 1), (ROWS, WF, WH, ROWS_PER_TILE * DIRECT_H))[part]
            by_row = keep.tile([COLS, 2, NH, width], F32, name="by_row%d_%d" % (m, part))
            shape = [COLS, 2, NH, width]
            nc.gpsimd.tensor_tensor(
                out=by_row[:],
                in0=gain_sb[m][:, :, col : col + width].unsqueeze(1).broadcast_to(shape),
                in1=cs[0:COLS, :, ANG_ALL + col : ANG_ALL + col + width].unsqueeze(2).broadcast_to(shape),
                op=ALU.mult,
            )
            size = 2 * NH * width
            offset = (2 * part + m) * ROWS * 2 * NH * WF
            parked[m, part] = park[offset : offset + rows * size].rearrange("(r n) -> r n", n=size)
            nc.sync.dma_start(out=parked[m, part][lo:rows, :], in_=by_row[lo:rows].rearrange("p c h n -> p (c h n)"))

        def spread_row_tables(m):
            tabs = keep.tile([P, ROW_GROUPS - DIRECT_H, 2, NH, WH], F32, name="row_tabs%d" % m)
            for r in range(ROWS_PER_TILE):
                nc.sync.dma_start(
                    out=tabs[COLS * r : COLS * (r + 1)].rearrange("p v c h n -> p v (c h n)"),
                    in_=parked[m, 1][ROWS_PER_TILE * DIRECT_H + r : ROWS : ROWS_PER_TILE, :].partition_broadcast(COLS),
                )
            for v in range(DIRECT_H, ROW_GROUPS):
                tables[m, 1, v] = tabs[:, v - DIRECT_H]

        def spread_frame_table(m, f):
            tab = keep.tile([P, 2, NH, WF], F32, name="frame_tab%d_%d" % (m, f))
            nc.sync.dma_start(
                out=tab[:].rearrange("p c h n -> p (c h n)"), in_=parked[m, 0][f, :].partition_broadcast(P)
            )
            tables[m, 0, f] = tab

        for m in range(2):
            nc.vector.tensor_copy(out=gain_sb[m][:], in_=gain[m][0:COLS, :, 0 : WF + WH])
            if m == 1 and first == 1:
                quantise(1)
            for part, variant in [(2, 0), (0, 0)] + [(1, r) for r in range(DIRECT_H)]:
                make_table(nc.vector, gain[m], m, part, variant)
            park_rows(m, 1)
        for m in range(2):
            spread_row_tables(m)
        for m in range(2):
            park_rows(m, 0)
        for i in range(4, BLOCKS):
            nc.sync.dma_start(out=x_sb[i][:], in_=x_rows[i])

        x_at, quantise_at = {}, {}
        for i in range(1, BLOCKS):
            first_fill = 2 * BLOCK_START[i] - BLOCK_TILES[i - 1]
            for j in range(BLOCK_TILES[i]):
                x_at[first_fill - 1 - BLOCK_TILES[i] + j] = BLOCK_START[i] + j
            quantise_at[first_fill - 2] = i

        for step in range(UNITS + 1):
            fills = []
            if step < UNITS:
                group, j, t, m = unit_place(step)
                nxt = group + 1
                if nxt < 2 * BLOCKS:
                    count, steps = 2 * BLOCK_TILES[nxt // 2], BLOCK_TILES[group // 2]
                    fills = list(range(count * j // steps, count * (j + 1) // steps))
            accs = [project(nxt, fill) for fill in fills[:2]]
            xt = transpose_x(x_at[step]) if step in x_at else None
            if step < UNITS:
                transpose_z(step)
            on_vector = xt is not None and x_at[step] in range(2, 16)
            if fills:
                add_bias(nxt, fills[0], accs[0], slice(0, 1))
            elif step < UNITS:
                mean_square(step, 0)
            if step > 0:
                add_halves(step - 1)
            if fills:
                add_bias(nxt, fills[0], accs[0], slice(1, None))
            if step > 0:
                inverse_rms(step - 1)
            if len(fills) > 1:
                add_bias(nxt, fills[1], accs[1])
            if xt is not None:
                copy_x(x_at[step], xt, passes=slice(0, 1 if on_vector else PASSES))
            if step < UNITS:
                if fills:
                    mean_square(step, 0)
                mean_square(step, 1)
            for fill in fills[2:]:
                add_bias(nxt, fill, project(nxt, fill))
            if step > 0:
                rope_terms(step - 1, 0, 0)
                rope_terms(step - 1, 0, 1)
            if on_vector:
                copy_x(x_at[step], xt, nc.vector.tensor_copy, slice(1, PASSES))
            if step > 0:
                rope_terms(step - 1, 1, 0)

            if step > 0:
                rope_terms(step - 1, 1, 1)
            if step in quantise_at:
                quantise(quantise_at[step])
            if 0 < step < UNITS:
                finish(nc.gpsimd, step - 1, 0, NH)
            if 1 <= step < 1 + 2 * (FRAMES - 1):
                spread_frame_table((step - 1) % 2, 1 + (step - 1) // 2)
        finish(nc.vector, UNITS - 1, 0, NH // 2)
        finish(nc.vector, UNITS - 1, NH // 2, NH)
